import numpy as np
import ml_dtypes


def mxq(x, axis, fmt="e4m3"):
    dtype, down = {"e4m3": (ml_dtypes.float8_e4m3fn, 7), "e5m2": (ml_dtypes.float8_e5m2, 14)}[fmt]
    v = np.moveaxis(np.asarray(x, np.float32).astype(ml_dtypes.bfloat16).astype(np.float64), axis, -1)
    blocks = v.reshape(v.shape[:-1] + (-1, 32))
    amax = np.abs(blocks).max(-1, keepdims=True)
    byte = np.maximum(np.where(amax > 0, np.frexp(amax)[1] - 1 + 127, 0) - down, 1)
    scale = np.exp2(byte - 127.0)
    codes = (blocks / scale).astype(np.float32).astype(dtype).astype(np.float64)
    return np.moveaxis((codes * scale).reshape(v.shape), -1, axis)


WIDE = False


def mx_kscale(k):
    if not WIDE:
        return np.ones(k)
    levels = np.array([10, -10, 5, -5, 0])
    a = np.random.permutation(np.resize(levels, k // 512 * 4)).reshape(k // 512, 4)
    idx = np.arange(k)
    return np.exp2(a[idx // 512, idx % 128 // 32])


BF16 = ml_dtypes.bfloat16


def bf(x):
    return np.asarray(x, np.float32).astype(BF16)


def f64(x):
    return np.asarray(x).astype(np.float64)


BATCH, IN_Q, OUT_Q = 8192, 256, 128
K, N = 4 * IN_Q, 4 * OUT_Q


def _quat_block_matrix(W):
    Ww, Wx, Wy, Wz = W[..., 0], W[..., 1], W[..., 2], W[..., 3]
    row_w = np.stack([Ww, -Wx, -Wy, -Wz], axis=0)
    row_x = np.stack([Wx, Ww, -Wz, Wy], axis=0)
    row_y = np.stack([Wy, Wz, Ww, -Wx], axis=0)
    row_z = np.stack([Wz, -Wy, Wx, Ww], axis=0)
    return np.stack([row_w, row_x, row_y, row_z], axis=0)


def setup_inputs():
    s = mx_kscale(K)[::4]
    sigma = 1.0 / np.sqrt(2.0 * (IN_Q + OUT_Q))
    return {"x": bf(np.random.standard_normal((BATCH, IN_Q, 4)) * s[None, :, None]),
            "W": bf(np.random.standard_normal((OUT_Q, IN_Q, 4)) * sigma / s[None, :, None]),
            "B": bf(np.random.standard_normal((OUT_Q, 4)) * 0.2)}


def reference(x, W, B):
    Wq = mxq(f64(W).reshape(OUT_Q, K), 1, "e4m3").reshape(OUT_Q, IN_Q, 4)
    M = _quat_block_matrix(Wq)
    Mk = M.transpose(3, 1, 2, 0).reshape(K, N)
    xk = f64(x).reshape(BATCH, K)
    s = (mxq(xk, 1, "e4m3") @ Mk).reshape(BATCH, OUT_Q, 4)
    s = s + f64(B)
    return np.tanh(s)

@@ -1,0 +1,246 @@
+from contextlib import ExitStack
+
+import concourse.mybir as mybir
+from concourse.masks import make_identity
+
+F32 = mybir.dt.float32
+BF16 = mybir.dt.bfloat16
+U32 = mybir.dt.uint32
+U8 = mybir.dt.uint8
+FP8X4 = mybir.dt.float8_e4m3fn_x4
+ACT = mybir.ActivationFunctionType
+ALU = mybir.AluOpType
+
+P = 128
+BATCH, IN_Q, OUT_Q = 8192, 256, 128
+K, N = 4 * IN_Q, 4 * OUT_Q
+FLOPS = 2 * BATCH * K * N
+ROW_TILES = BATCH // P
+R = 4
+GROUPS = ROW_TILES // R
+HEAD_CHUNKS = [1, 1, 2, 4]
+MAIN_CHUNK = 8
+MAIN_BUFS = 6
+
+PLACE = [
+    (0, 0, 1, 1, 0, 1.0),
+    (0, 1, 3, 1, 1, -1.0),
+    (1, 1, 2, 2, 0, 1.0),
+    (1, 0, 1, 1, 1, 1.0),
+    (1, 2, 1, 1, 3, -1.0),
+    (2, 0, 2, 1, 2, 1.0),
+    (2, 2, 1, 1, 0, 1.0),
+    (2, 3, 1, 1, 1, -1.0),
+    (3, 0, 1, 1, 3, 1.0),
+    (3, 1, 1, 1, 2, -1.0),
+    (3, 2, 1, 1, 1, 1.0),
+    (3, 3, 1, 1, 0, 1.0),
+]
+
+
+def vector_copies(j, r):
+    return r == R - 1 and j % 4 != 3
+
+
+def tile_quatnetpytorchdenselayer_t_kernel(tc, x, W, B, out):
+    nc = tc.nc
+    xv = x.rearrange("(p t) i c -> p t (i c)", t=ROW_TILES)
+    ov = out.rearrange("(p t) o d -> p t (o d)", t=ROW_TILES)
+
+    with ExitStack() as ctx:
+        const = ctx.enter_context(tc.tile_pool(name="const", bufs=1))
+        xhead = ctx.enter_context(tc.tile_pool(name="xhead", bufs=1))
+        xmain = ctx.enter_context(tc.tile_pool(name="xmain", bufs=MAIN_BUFS))
+        gpool = ctx.enter_context(tc.tile_pool(name="gpool", bufs=3))
+        cpool = ctx.enter_context(tc.tile_pool(name="cpool", bufs=3))
+        opool = ctx.enter_context(tc.tile_pool(name="opool", bufs=4))
+        ps_t = ctx.enter_context(tc.psum_pool(name="ps_t", bufs=4))
+        ps_o = ctx.enter_context(tc.psum_pool(name="ps_o", bufs=4))
+
+        warm = const.tile([P, 1], F32, name="warm")
+        nc.vector.memset(warm[:], 0.0)
+        b_row = const.tile([P, N], BF16, name="b_row")
+        nc.vector.memset(b_row[:], 0.0)
+        ones = const.tile([P, P], BF16, name="ones")
+        nc.vector.memset(ones[:], 1.0)
+        nc.scalar.activation(out=warm[:], in_=warm[:], func=ACT.Tanh)
+        ident = const.tile([P, P], F32, name="ident")
+        make_identity(nc, ident[:])
+
+        w_sb = const.tile([P, IN_Q, 4], BF16, name="w_sb")
+        nc.sync.dma_start(out=w_sb[:], in_=W)
+
+        chunks = []
+        t0 = 0
+        for n_rows in HEAD_CHUNKS:
+            chunks.append((t0, n_rows))
+            t0 += n_rows
+        while t0 < ROW_TILES:
+            chunks.append((t0, MAIN_CHUNK))
+            t0 += MAIN_CHUNK
+        where = {}
+
+        def load_chunk(ci):
+            first, n_rows = chunks[ci]
+            if ci < len(HEAD_CHUNKS):
+                xs = xhead.tile([P, n_rows, K], BF16, name="xh%d" % ci)
+            else:
+                xs = xmain.tile([P, MAIN_CHUNK, K], BF16, name="xs", tag="xs")
+            nc.sync.dma_start(out=xs[:], in_=xv[:, first : first + n_rows, :])
+            words = xs[:].bitcast(F32)
+            for r in range(n_rows):
+                where[first + r] = (words, r)
+
+        n_first = len(HEAD_CHUNKS) + MAIN_BUFS
+        for ci in range(min(n_first, len(chunks))):
+            load_chunk(ci)
+            if ci == 2:
+                nc.sync.dma_start(out=b_row[0:1, :], in_=B.rearrange("(a o) d -> a (o d)", a=1))
+        last_of_chunk = {}
+        for ci in range(len(HEAD_CHUNKS), len(chunks)):
+            last_of_chunk[chunks[ci][0] + chunks[ci][1] - 1] = ci
+
+        banks = {}
+        grouped = {}
+        codes = {}
+        planes = {}
+        accs = {}
+        outs = {}
+
+        def transposes(j):
+            for r in range(R):
+                words, idx = where[j * R + r]
+                xt = ps_t.tile([P, 4, P], F32, name="xt", tag="xt")
+                for q in range(4):
+                    nc.tensor.transpose(xt[:, q, :], words[:, idx, q * P : (q + 1) * P], ident[:])
+                banks[(j, r)] = xt
+                ci = last_of_chunk.get(j * R + r)
+                if ci is not None and ci + MAIN_BUFS < len(chunks):
+                    load_chunk(ci + MAIN_BUFS)
+
+        def copies(j, on_vector):
+            if j not in grouped:
+                grouped[j] = gpool.tile([P, R * K], BF16, name="grp", tag="grp", align_bytes=64)
+            gw = grouped[j][:].bitcast(F32).rearrange("p (r g b u) -> p r g b u", r=R, g=2, u=2)
+            for r in range(R):
+                if vector_copies(j, r) != on_vector:
+                    continue
+                src = banks[(j, r)][:].rearrange("p (g u) b -> p g b u", u=2)
+                if on_vector:
+                    nc.vector.tensor_copy(out=gw[:, r], in_=src)
+                else:
+                    nc.scalar.copy(out=gw[:, r], in_=src)
+
+        def quantise(j):
+            cw = cpool.tile([P, R * 2 * P], U32, name="cw", tag="cw", align_bytes=64)
+            sc = cpool.tile([P, R * 2 * P], U8, name="sc", tag="sc", align_bytes=64)
+            nc.vector.quantize_mx(out=cw[:].bitcast(FP8X4), scales=sc[:], in_=grouped[j][:])
+            codes[j] = cw
+            planes[j] = sc
+
+        def passes(j):
+            for r in range(R):
+                acc = ps_o.tile([P, N], F32, name="acc", tag="acc")
+                for g in range(2):
+                    col = (2 * r + g) * P
+                    nc.tensor.matmul_mx(
+                        out=acc[:],
+                        lhsT=codes[j][:, col : col + P].bitcast(FP8X4),
+                        lhsT_scale=planes[j][:, col : col + P],
+                        rhs=mk_codes[:, g * N : (g + 1) * N].bitcast(FP8X4),
+                        rhs_scale=mk_planes[:, g * N : (g + 1) * N],
+                        start=(g == 0),
+                        stop=(g == 1),
+                    )
+                accs[(j, r)] = acc
+
+        def adds(j, rows):
+            if j not in outs:
+                outs[j] = opool.tile([P, R, N], F32, name="ot", tag="ot")
+            for r in rows:
+                nc.vector.tensor_tensor(out=outs[j][:, r, :], in0=accs[(j, r)][:], in1=bias[:], op=ALU.add)
+
+        def finish(j, r0, r1):
+            part = outs[j][:, r0:r1, :]
+            nc.scalar.activation(out=part, in_=part, func=ACT.Tanh)
+            nc.scalar.dma_start(out=ov[:, j * R + r0 : j * R + r1, :], in_=part)
+
+        mk_t = const.tile([P, 4, K], BF16, name="mk_t")
+        mk_v = mk_t[:].rearrange("p d (i c) -> p d i c", c=4)
+        for d, c_out, n_c, step, c_in, sign in PLACE:
+            dst = mk_v[:, d, :, c_out : c_out + (n_c - 1) * step + 1 : step]
+            src = w_sb[:, :, c_in : c_in + (n_c - 1) * step + 1 : step]
+            if d < 2:
+                nc.vector.tensor_scalar(out=dst, in0=src, scalar1=sign, scalar2=None, op0=ALU.mult)
+            elif d == 2:
+                nc.scalar.mul(out=dst, in_=src, mul=sign)
+            else:
+                nc.gpsimd.tensor_scalar(out=dst, in0=src, scalar1=sign, scalar2=0.0, op0=ALU.mult, op1=ALU.add)
+
+        transposes(0)
+        copies(0, False)
+        copies(0, True)
+
+        pb = ps_o.tile([P, N], F32, name="acc", tag="acc")
+        nc.tensor.matmul(out=pb[:], lhsT=ones[:], rhs=b_row[:], start=True, stop=True)
+        bias = const.tile([P, N], F32, name="bias")
+        nc.vector.tensor_copy(out=bias[:], in_=pb[:])
+
+        mk_w = mk_t[:].bitcast(F32)
+        mk_g = const.tile([P, 2, 4 * N], BF16, name="mk_g", align_bytes=64)
+        mk_gw = mk_g[:].bitcast(F32).rearrange("p g (o d u) -> p g o d u", d=4, u=2)
+        mk_codes = const.tile([P, 2 * N], U32, name="mk_codes", align_bytes=64)
+        mk_planes = const.tile([P, 2 * N], U8, name="mk_planes", align_bytes=64)
+        mk_banks = {}
+        for dh in range(2):
+            for g in range(2):
+                pm = ps_o.tile([P, 4, P], F32, name="acc", tag="acc")
+                for dl in range(2):
+                    for u in range(2):
+                        first = (2 * g + u) * P
+                        nc.tensor.transpose(pm[:, 2 * dl + u, :], mk_w[:, 2 * dh + dl, first : first + P], ident[:])
+                mk_banks[(g, dh)] = pm
+
+        def mk_exit(g, dh):
+            dst = mk_gw[:, g, :, 2 * dh : 2 * dh + 2, :]
+            src = mk_banks[(g, dh)][:].rearrange("p (l u) o -> p o l u", u=2)
+            if g == 0:
+                nc.vector.tensor_copy(out=dst, in_=src)
+            else:
+                nc.scalar.copy(out=dst, in_=src)
+
+        mk_exit(0, 0)
+        mk_exit(1, 0)
+        transposes(1)
+        quantise(0)
+        mk_exit(0, 1)
+        mk_exit(1, 1)
+        copies(1, False)
+        for g in range(2):
+            nc.vector.quantize_mx(
+                out=mk_codes[:, g * N : (g + 1) * N].bitcast(FP8X4),
+                scales=mk_planes[:, g * N : (g + 1) * N],
+                in_=mk_g[:, g, :],
+            )
+        copies(1, True)
+
+        for s in range(2, GROUPS + 2):
+            if s < GROUPS:
+                transposes(s)
+            passes(s - 2)
+            if s < GROUPS:
+                copies(s, False)
+            if s <= GROUPS:
+                quantise(s - 1)
+            if s < GROUPS:
+                copies(s, True)
+            if s - 2 < GROUPS - 1:
+                adds(s - 2, range(R))
+                if s >= 3:
+                    finish(s - 3, 0, R)
+            else:
+                finish(s - 3, 0, R)
+                adds(s - 2, range(0, 2))
+                finish(s - 2, 0, 2)
+                adds(s - 2, range(2, 4))
+                finish(s - 2, 2, 4)

@@ -20,7 +20,7 @@ R = 4
 GROUPS = ROW_TILES // R
 HEAD_CHUNKS = [1, 1, 2, 4]
 MAIN_CHUNK = 8
-MAIN_BUFS = 6
+MAIN_BUFS = 4
 
 PLACE = [
     (0, 0, 1, 1, 0, 1.0),
@@ -53,7 +53,7 @@ def tile_quatnetpytorchdenselayer_t_kernel(tc, x, W, B, out):
         xmain = ctx.enter_context(tc.tile_pool(name="xmain", bufs=MAIN_BUFS))
         gpool = ctx.enter_context(tc.tile_pool(name="gpool", bufs=3))
         cpool = ctx.enter_context(tc.tile_pool(name="cpool", bufs=3))
-        opool = ctx.enter_context(tc.tile_pool(name="opool", bufs=4))
+        opool = ctx.enter_context(tc.tile_pool(name="opool", bufs=5))
         ps_t = ctx.enter_context(tc.psum_pool(name="ps_t", bufs=4))
         ps_o = ctx.enter_context(tc.psum_pool(name="ps_o", bufs=4))
 
@@ -163,7 +163,7 @@ def tile_quatnetpytorchdenselayer_t_kernel(tc, x, W, B, out):
         def finish(j, r0, r1):
             part = outs[j][:, r0:r1, :]
             nc.scalar.activation(out=part, in_=part, func=ACT.Tanh)
-            nc.scalar.dma_start(out=ov[:, j * R + r0 : j * R + r1, :], in_=part)
+            nc.gpsimd.dma_start(out=ov[:, j * R + r0 : j * R + r1, :], in_=part)
 
         mk_t = const.tile([P, 4, K], BF16, name="mk_t")
         mk_v = mk_t[:].rearrange("p d (i c) -> p d i c", c=4)

@@ -16,11 +16,16 @@ BATCH, IN_Q, OUT_Q = 8192, 256, 128
 K, N = 4 * IN_Q, 4 * OUT_Q
 FLOPS = 2 * BATCH * K * N
 ROW_TILES = BATCH // P
-R = 4
+R = 2
 GROUPS = ROW_TILES // R
+STORE_GROUPS = 2
 HEAD_CHUNKS = [1, 1, 2, 4]
 MAIN_CHUNK = 8
 MAIN_BUFS = 4
+LAG_MX = 3
+LAG_ADD = 4
+LAG_TANH = 5
+SYNC_STORES = 2
 
 PLACE = [
     (0, 0, 1, 1, 0, 1.0),
@@ -39,7 +44,7 @@ PLACE = [
 
 
 def vector_copies(j, r):
-    return r == R - 1 and j % 4 != 3
+    return r == R - 1 and j % 8 in (1, 4, 6)
 
 
 def tile_quatnetpytorchdenselayer_t_kernel(tc, x, W, B, out):
@@ -52,10 +57,11 @@ def tile_quatnetpytorchdenselayer_t_kernel(tc, x, W, B, out):
         xhead = ctx.enter_context(tc.tile_pool(name="xhead", bufs=1))
         xmain = ctx.enter_context(tc.tile_pool(name="xmain", bufs=MAIN_BUFS))
         gpool = ctx.enter_context(tc.tile_pool(name="gpool", bufs=3))
-        cpool = ctx.enter_context(tc.tile_pool(name="cpool", bufs=3))
+        cpool = ctx.enter_context(tc.tile_pool(name="cpool", bufs=LAG_MX + 2))
         opool = ctx.enter_context(tc.tile_pool(name="opool", bufs=5))
         ps_t = ctx.enter_context(tc.psum_pool(name="ps_t", bufs=4))
         ps_o = ctx.enter_context(tc.psum_pool(name="ps_o", bufs=4))
+        ctx.enter_context(tc.manual_schedule())
 
         warm = const.tile([P, 1], F32, name="warm")
         nc.vector.memset(warm[:], 0.0)
@@ -118,15 +124,13 @@ def tile_quatnetpytorchdenselayer_t_kernel(tc, x, W, B, out):
                 if ci is not None and ci + MAIN_BUFS < len(chunks):
                     load_chunk(ci + MAIN_BUFS)
 
-        def copies(j, on_vector):
-            if j not in grouped:
-                grouped[j] = gpool.tile([P, R * K], BF16, name="grp", tag="grp", align_bytes=64)
-            gw = grouped[j][:].bitcast(F32).rearrange("p (r g b u) -> p r g b u", r=R, g=2, u=2)
+        def copies(j):
+            grp = gpool.tile([P, R * K], BF16, name="grp", tag="grp", align_bytes=64)
+            grouped[j] = grp
+            gw = grp[:].bitcast(F32).rearrange("p (r g b u) -> p r g b u", r=R, g=2, u=2)
             for r in range(R):
-                if vector_copies(j, r) != on_vector:
-                    continue
                 src = banks[(j, r)][:].rearrange("p (g u) b -> p g b u", u=2)
-                if on_vector:
+                if vector_copies(j, r):
                     nc.vector.tensor_copy(out=gw[:, r], in_=src)
                 else:
                     nc.scalar.copy(out=gw[:, r], in_=src)
@@ -154,16 +158,26 @@ def tile_quatnetpytorchdenselayer_t_kernel(tc, x, W, B, out):
                     )
                 accs[(j, r)] = acc
 
-        def adds(j, rows):
-            if j not in outs:
-                outs[j] = opool.tile([P, R, N], F32, name="ot", tag="ot")
-            for r in rows:
-                nc.vector.tensor_tensor(out=outs[j][:, r, :], in0=accs[(j, r)][:], in1=bias[:], op=ALU.add)
+        def adds(j):
+            big, half = divmod(j, STORE_GROUPS)
+            if half == 0:
+                outs[big] = opool.tile([P, STORE_GROUPS * R, N], F32, name="ot", tag="ot")
+            for r in range(R):
+                nc.vector.tensor_tensor(out=outs[big][:, half * R + r, :], in0=accs[(j, r)][:], in1=bias[:], op=ALU.add)
 
-        def finish(j, r0, r1):
-            part = outs[j][:, r0:r1, :]
+        def finish(j):
+            big, half = divmod(j, STORE_GROUPS)
+            part = outs[big][:, half * R : (half + 1) * R, :]
             nc.scalar.activation(out=part, in_=part, func=ACT.Tanh)
-            nc.gpsimd.dma_start(out=ov[:, j * R + r0 : j * R + r1, :], in_=part)
+            n_big = GROUPS // STORE_GROUPS
+            if big == n_big - 1:
+                nc.sync.dma_start(out=ov[:, j * R : (j + 1) * R, :], in_=part)
+            elif half == STORE_GROUPS - 1:
+                rows = ov[:, big * STORE_GROUPS * R : (big + 1) * STORE_GROUPS * R, :]
+                if big >= n_big - SYNC_STORES:
+                    nc.sync.dma_start(out=rows, in_=outs[big][:])
+                else:
+                    nc.gpsimd.dma_start(out=rows, in_=outs[big][:])
 
         mk_t = const.tile([P, 4, K], BF16, name="mk_t")
         mk_v = mk_t[:].rearrange("p d (i c) -> p d i c", c=4)
@@ -178,8 +192,9 @@ def tile_quatnetpytorchdenselayer_t_kernel(tc, x, W, B, out):
                 nc.gpsimd.tensor_scalar(out=dst, in0=src, scalar1=sign, scalar2=0.0, op0=ALU.mult, op1=ALU.add)
 
         transposes(0)
-        copies(0, False)
-        copies(0, True)
+        copies(0)
+        transposes(1)
+        copies(1)
 
         pb = ps_o.tile([P, N], F32, name="acc", tag="acc")
         nc.tensor.matmul(out=pb[:], lhsT=ones[:], rhs=b_row[:], start=True, stop=True)
@@ -209,38 +224,28 @@ def tile_quatnetpytorchdenselayer_t_kernel(tc, x, W, B, out):
             else:
                 nc.scalar.copy(out=dst, in_=src)
 
+        quantise(0)
         mk_exit(0, 0)
         mk_exit(1, 0)
-        transposes(1)
-        quantise(0)
         mk_exit(0, 1)
         mk_exit(1, 1)
-        copies(1, False)
         for g in range(2):
             nc.vector.quantize_mx(
                 out=mk_codes[:, g * N : (g + 1) * N].bitcast(FP8X4),
                 scales=mk_planes[:, g * N : (g + 1) * N],
                 in_=mk_g[:, g, :],
             )
-        copies(1, True)
 
-        for s in range(2, GROUPS + 2):
+        for s in range(2, GROUPS + LAG_TANH):
             if s < GROUPS:
                 transposes(s)
-            passes(s - 2)
+            if 0 <= s - LAG_MX < GROUPS:
+                passes(s - LAG_MX)
+            if 0 <= s - LAG_ADD < GROUPS:
+                adds(s - LAG_ADD)
+            if 0 <= s - LAG_TANH < GROUPS:
+                finish(s - LAG_TANH)
             if s < GROUPS:
-                copies(s, False)
-            if s <= GROUPS:
+                copies(s)
+            if s - 1 < GROUPS:
                 quantise(s - 1)
-            if s < GROUPS:
-                copies(s, True)
-            if s - 2 < GROUPS - 1:
-                adds(s - 2, range(R))
-                if s >= 3:
-                    finish(s - 3, 0, R)
-            else:
-                finish(s - 3, 0, R)
-                adds(s - 2, range(0, 2))
-                finish(s - 2, 0, 2)
-                adds(s - 2, range(2, 4))
-                finish(s - 2, 2, 4)

@@ -44,7 +44,7 @@ PLACE = [
 
 
 def vector_copies(j, r):
-    return r == R - 1 and j % 8 in (1, 4, 6)
+    return r == R - 1 and j % 8 == 4
 
 
 def tile_quatnetpytorchdenselayer_t_kernel(tc, x, W, B, out):

@@ -19,13 +19,17 @@ ROW_TILES = BATCH // P
 R = 2
 GROUPS = ROW_TILES // R
 STORE_GROUPS = 2
-HEAD_CHUNKS = [1, 1, 2, 4]
+HEAD_CHUNKS = [1, 1, 2, 4, 4, 4]
 MAIN_CHUNK = 8
 MAIN_BUFS = 4
 LAG_MX = 3
 LAG_ADD = 4
 LAG_TANH = 5
-SYNC_STORES = 2
+OUT_TILES = STORE_GROUPS * R
+SYNC_FROM = 48
+FINE_FROM = 52
+SPLIT_FROM = 56
+WARM_FIRST = 5
 
 PLACE = [
     (0, 0, 1, 1, 0, 1.0),
@@ -44,7 +48,7 @@ PLACE = [
 
 
 def vector_copies(j, r):
-    return r == R - 1 and j % 8 == 4
+    return r == R - 1 and j % 8 in (1, 4, 6)
 
 
 def tile_quatnetpytorchdenselayer_t_kernel(tc, x, W, B, out):
@@ -63,12 +67,14 @@ def tile_quatnetpytorchdenselayer_t_kernel(tc, x, W, B, out):
         ps_o = ctx.enter_context(tc.psum_pool(name="ps_o", bufs=4))
         ctx.enter_context(tc.manual_schedule())
 
+        ones = const.tile([P, P], BF16, name="ones")
+        nc.vector.memset(ones[:], 1.0)
+        zeros = const.tile([P, N], BF16, name="zeros")
+        nc.vector.memset(zeros[:], 0.0)
         warm = const.tile([P, 1], F32, name="warm")
         nc.vector.memset(warm[:], 0.0)
         b_row = const.tile([P, N], BF16, name="b_row")
         nc.vector.memset(b_row[:], 0.0)
-        ones = const.tile([P, P], BF16, name="ones")
-        nc.vector.memset(ones[:], 1.0)
         nc.scalar.activation(out=warm[:], in_=warm[:], func=ACT.Tanh)
         ident = const.tile([P, P], F32, name="ident")
         make_identity(nc, ident[:])
@@ -113,10 +119,16 @@ def tile_quatnetpytorchdenselayer_t_kernel(tc, x, W, B, out):
         accs = {}
         outs = {}
 
-        def transposes(j):
+        def keep_clock(bank, times):
+            for i_warm in range(times):
+                nc.tensor.matmul(out=bank[:].rearrange("p q b -> p (q b)"), lhsT=ones[:], rhs=zeros[:], start=True, stop=True)
+
+        def transposes(j, warmers=0):
             for r in range(R):
                 words, idx = where[j * R + r]
                 xt = ps_t.tile([P, 4, P], F32, name="xt", tag="xt")
+                if r == 0:
+                    keep_clock(xt, warmers)
                 for q in range(4):
                     nc.tensor.transpose(xt[:, q, :], words[:, idx, q * P : (q + 1) * P], ident[:])
                 banks[(j, r)] = xt
@@ -166,18 +178,17 @@ def tile_quatnetpytorchdenselayer_t_kernel(tc, x, W, B, out):
                 nc.vector.tensor_tensor(out=outs[big][:, half * R + r, :], in0=accs[(j, r)][:], in1=bias[:], op=ALU.add)
 
         def finish(j):
-            big, half = divmod(j, STORE_GROUPS)
-            part = outs[big][:, half * R : (half + 1) * R, :]
-            nc.scalar.activation(out=part, in_=part, func=ACT.Tanh)
-            n_big = GROUPS // STORE_GROUPS
-            if big == n_big - 1:
-                nc.sync.dma_start(out=ov[:, j * R : (j + 1) * R, :], in_=part)
-            elif half == STORE_GROUPS - 1:
-                rows = ov[:, big * STORE_GROUPS * R : (big + 1) * STORE_GROUPS * R, :]
-                if big >= n_big - SYNC_STORES:
-                    nc.sync.dma_start(out=rows, in_=outs[big][:])
-                else:
-                    nc.gpsimd.dma_start(out=rows, in_=outs[big][:])
+            first = j * R
+            big, pos = divmod(first, OUT_TILES)
+            pieces = [(first + r, 1) for r in range(R)] if first >= SPLIT_FROM else [(first, R)]
+            for t, n_rows in pieces:
+                part = outs[big][:, t - big * OUT_TILES : t - big * OUT_TILES + n_rows, :]
+                nc.scalar.activation(out=part, in_=part, func=ACT.Tanh)
+                if t >= FINE_FROM:
+                    nc.sync.dma_start(out=ov[:, t : t + n_rows, :], in_=part)
+            if first < FINE_FROM and pos + R == OUT_TILES:
+                queue = nc.sync if first >= SYNC_FROM else nc.gpsimd
+                queue.dma_start(out=ov[:, big * OUT_TILES : (big + 1) * OUT_TILES, :], in_=outs[big][:])
 
         mk_t = const.tile([P, 4, K], BF16, name="mk_t")
         mk_v = mk_t[:].rearrange("p d (i c) -> p d i c", c=4)
@@ -191,15 +202,14 @@ def tile_quatnetpytorchdenselayer_t_kernel(tc, x, W, B, out):
             else:
                 nc.gpsimd.tensor_scalar(out=dst, in0=src, scalar1=sign, scalar2=0.0, op0=ALU.mult, op1=ALU.add)
 
-        transposes(0)
+        transposes(0, WARM_FIRST)
         copies(0)
-        transposes(1)
+        transposes(1, 1)
         copies(1)
 
         pb = ps_o.tile([P, N], F32, name="acc", tag="acc")
         nc.tensor.matmul(out=pb[:], lhsT=ones[:], rhs=b_row[:], start=True, stop=True)
         bias = const.tile([P, N], F32, name="bias")
-        nc.vector.tensor_copy(out=bias[:], in_=pb[:])
 
         mk_w = mk_t[:].bitcast(F32)
         mk_g = const.tile([P, 2, 4 * N], BF16, name="mk_g", align_bytes=64)
@@ -209,7 +219,11 @@ def tile_quatnetpytorchdenselayer_t_kernel(tc, x, W, B, out):
         mk_banks = {}
         for dh in range(2):
             for g in range(2):
+                if (g, dh) == (1, 1):
+                    nc.vector.tensor_copy(out=bias[:], in_=pb[:])
                 pm = ps_o.tile([P, 4, P], F32, name="acc", tag="acc")
+                if (g, dh) == (0, 1):
+                    keep_clock(pm, 1)
                 for dl in range(2):
                     for u in range(2):
                         first = (2 * g + u) * P
@@ -224,9 +238,9 @@ def tile_quatnetpytorchdenselayer_t_kernel(tc, x, W, B, out):
             else:
                 nc.scalar.copy(out=dst, in_=src)
 
-        quantise(0)
         mk_exit(0, 0)
         mk_exit(1, 0)
+        quantise(0)
         mk_exit(0, 1)
         mk_exit(1, 1)
         for g in range(2):
@@ -238,7 +252,7 @@ def tile_quatnetpytorchdenselayer_t_kernel(tc, x, W, B, out):
 
         for s in range(2, GROUPS + LAG_TANH):
             if s < GROUPS:
-                transposes(s)
+                transposes(s, 1 if s <= LAG_MX else 0)
             if 0 <= s - LAG_MX < GROUPS:
                 passes(s - LAG_MX)
             if 0 <= s - LAG_ADD < GROUPS:

@@ -29,7 +29,9 @@ OUT_TILES = STORE_GROUPS * R
 SYNC_FROM = 48
 FINE_FROM = 52
 SPLIT_FROM = 56
-WARM_FIRST = 5
+WARMERS = {0: 8, 1: 1, 2: 3, 4: 1, 6: 1}
+WARM_MK = 1
+WARM_MX = 2
 
 PLACE = [
     (0, 0, 1, 1, 0, 1.0),
@@ -121,14 +123,13 @@ def tile_quatnetpytorchdenselayer_t_kernel(tc, x, W, B, out):
 
         def keep_clock(bank, times):
             for i_warm in range(times):
-                nc.tensor.matmul(out=bank[:].rearrange("p q b -> p (q b)"), lhsT=ones[:], rhs=zeros[:], start=True, stop=True)
+                nc.tensor.matmul(out=bank, lhsT=ones[:], rhs=zeros[:], start=True, stop=True)
 
-        def transposes(j, warmers=0):
+        def transposes(j):
             for r in range(R):
                 words, idx = where[j * R + r]
                 xt = ps_t.tile([P, 4, P], F32, name="xt", tag="xt")
-                if r == 0:
-                    keep_clock(xt, warmers)
+                keep_clock(xt[:].rearrange("p q b -> p (q b)"), WARMERS.get(j * R + r, 0))
                 for q in range(4):
                     nc.tensor.transpose(xt[:, q, :], words[:, idx, q * P : (q + 1) * P], ident[:])
                 banks[(j, r)] = xt
@@ -157,6 +158,8 @@ def tile_quatnetpytorchdenselayer_t_kernel(tc, x, W, B, out):
         def passes(j):
             for r in range(R):
                 acc = ps_o.tile([P, N], F32, name="acc", tag="acc")
+                if j == 0 and r == 0:
+                    keep_clock(acc[:], WARM_MX)
                 for g in range(2):
                     col = (2 * r + g) * P
                     nc.tensor.matmul_mx(
@@ -202,9 +205,9 @@ def tile_quatnetpytorchdenselayer_t_kernel(tc, x, W, B, out):
             else:
                 nc.gpsimd.tensor_scalar(out=dst, in0=src, scalar1=sign, scalar2=0.0, op0=ALU.mult, op1=ALU.add)
 
-        transposes(0, WARM_FIRST)
+        transposes(0)
         copies(0)
-        transposes(1, 1)
+        transposes(1)
         copies(1)
 
         pb = ps_o.tile([P, N], F32, name="acc", tag="acc")
@@ -223,7 +226,7 @@ def tile_quatnetpytorchdenselayer_t_kernel(tc, x, W, B, out):
                     nc.vector.tensor_copy(out=bias[:], in_=pb[:])
                 pm = ps_o.tile([P, 4, P], F32, name="acc", tag="acc")
                 if (g, dh) == (0, 1):
-                    keep_clock(pm, 1)
+                    keep_clock(pm[:].rearrange("p q b -> p (q b)"), WARM_MK)
                 for dl in range(2):
                     for u in range(2):
                         first = (2 * g + u) * P
@@ -252,7 +255,7 @@ def tile_quatnetpytorchdenselayer_t_kernel(tc, x, W, B, out):
 
         for s in range(2, GROUPS + LAG_TANH):
             if s < GROUPS:
-                transposes(s, 1 if s <= LAG_MX else 0)
+                transposes(s)
             if 0 <= s - LAG_MX < GROUPS:
                 passes(s - LAG_MX)
             if 0 <= s - LAG_ADD < GROUPS:

@@ -29,9 +29,7 @@ OUT_TILES = STORE_GROUPS * R
 SYNC_FROM = 48
 FINE_FROM = 52
 SPLIT_FROM = 56
-WARMERS = {0: 8, 1: 1, 2: 3, 4: 1, 6: 1}
-WARM_MK = 1
-WARM_MX = 2
+WARM_FIRST = 5
 
 PLACE = [
     (0, 0, 1, 1, 0, 1.0),
@@ -62,9 +60,9 @@ def tile_quatnetpytorchdenselayer_t_kernel(tc, x, W, B, out):
         const = ctx.enter_context(tc.tile_pool(name="const", bufs=1))
         xhead = ctx.enter_context(tc.tile_pool(name="xhead", bufs=1))
         xmain = ctx.enter_context(tc.tile_pool(name="xmain", bufs=MAIN_BUFS))
-        gpool = ctx.enter_context(tc.tile_pool(name="gpool", bufs=3))
-        cpool = ctx.enter_context(tc.tile_pool(name="cpool", bufs=LAG_MX + 2))
-        opool = ctx.enter_context(tc.tile_pool(name="opool", bufs=5))
+        gpool = ctx.enter_context(tc.tile_pool(name="gpool", bufs=4))
+        cpool = ctx.enter_context(tc.tile_pool(name="cpool", bufs=LAG_MX + 3))
+        opool = ctx.enter_context(tc.tile_pool(name="opool", bufs=8))
         ps_t = ctx.enter_context(tc.psum_pool(name="ps_t", bufs=4))
         ps_o = ctx.enter_context(tc.psum_pool(name="ps_o", bufs=4))
         ctx.enter_context(tc.manual_schedule())
@@ -123,13 +121,14 @@ def tile_quatnetpytorchdenselayer_t_kernel(tc, x, W, B, out):
 
         def keep_clock(bank, times):
             for i_warm in range(times):
-                nc.tensor.matmul(out=bank, lhsT=ones[:], rhs=zeros[:], start=True, stop=True)
+                nc.tensor.matmul(out=bank[:].rearrange("p q b -> p (q b)"), lhsT=ones[:], rhs=zeros[:], start=True, stop=True)
 
-        def transposes(j):
+        def transposes(j, warmers=0):
             for r in range(R):
                 words, idx = where[j * R + r]
                 xt = ps_t.tile([P, 4, P], F32, name="xt", tag="xt")
-                keep_clock(xt[:].rearrange("p q b -> p (q b)"), WARMERS.get(j * R + r, 0))
+                if r == 0:
+                    keep_clock(xt, warmers)
                 for q in range(4):
                     nc.tensor.transpose(xt[:, q, :], words[:, idx, q * P : (q + 1) * P], ident[:])
                 banks[(j, r)] = xt
@@ -158,8 +157,6 @@ def tile_quatnetpytorchdenselayer_t_kernel(tc, x, W, B, out):
         def passes(j):
             for r in range(R):
                 acc = ps_o.tile([P, N], F32, name="acc", tag="acc")
-                if j == 0 and r == 0:
-                    keep_clock(acc[:], WARM_MX)
                 for g in range(2):
                     col = (2 * r + g) * P
                     nc.tensor.matmul_mx(
@@ -205,9 +202,9 @@ def tile_quatnetpytorchdenselayer_t_kernel(tc, x, W, B, out):
             else:
                 nc.gpsimd.tensor_scalar(out=dst, in0=src, scalar1=sign, scalar2=0.0, op0=ALU.mult, op1=ALU.add)
 
-        transposes(0)
+        transposes(0, WARM_FIRST)
         copies(0)
-        transposes(1)
+        transposes(1, 1)
         copies(1)
 
         pb = ps_o.tile([P, N], F32, name="acc", tag="acc")
@@ -226,7 +223,7 @@ def tile_quatnetpytorchdenselayer_t_kernel(tc, x, W, B, out):
                     nc.vector.tensor_copy(out=bias[:], in_=pb[:])
                 pm = ps_o.tile([P, 4, P], F32, name="acc", tag="acc")
                 if (g, dh) == (0, 1):
-                    keep_clock(pm[:].rearrange("p q b -> p (q b)"), WARM_MK)
+                    keep_clock(pm, 1)
                 for dl in range(2):
                     for u in range(2):
                         first = (2 * g + u) * P
@@ -255,7 +252,7 @@ def tile_quatnetpytorchdenselayer_t_kernel(tc, x, W, B, out):
 
         for s in range(2, GROUPS + LAG_TANH):
             if s < GROUPS:
-                transposes(s)
+                transposes(s, 1 if s <= LAG_MX else 0)
             if 0 <= s - LAG_MX < GROUPS:
                 passes(s - LAG_MX)
             if 0 <= s - LAG_ADD < GROUPS:

@@ -26,7 +26,7 @@ LAG_MX = 3
 LAG_ADD = 4
 LAG_TANH = 5
 OUT_TILES = STORE_GROUPS * R
-SYNC_FROM = 48
+SYNC_FROM = 20
 FINE_FROM = 52
 SPLIT_FROM = 56
 WARM_FIRST = 5
@@ -48,7 +48,7 @@ PLACE = [
 
 
 def vector_copies(j, r):
-    return r == R - 1 and j % 8 in (1, 4, 6)
+    return r == R - 1 and j % 8 in (1, 4, 6) and j > 4
 
 
 def tile_quatnetpytorchdenselayer_t_kernel(tc, x, W, B, out):
@@ -195,10 +195,8 @@ def tile_quatnetpytorchdenselayer_t_kernel(tc, x, W, B, out):
         for d, c_out, n_c, step, c_in, sign in PLACE:
             dst = mk_v[:, d, :, c_out : c_out + (n_c - 1) * step + 1 : step]
             src = w_sb[:, :, c_in : c_in + (n_c - 1) * step + 1 : step]
-            if d < 2:
+            if d < 3:
                 nc.vector.tensor_scalar(out=dst, in0=src, scalar1=sign, scalar2=None, op0=ALU.mult)
-            elif d == 2:
-                nc.scalar.mul(out=dst, in_=src, mul=sign)
             else:
                 nc.gpsimd.tensor_scalar(out=dst, in0=src, scalar1=sign, scalar2=0.0, op0=ALU.mult, op1=ALU.add)
 

from contextlib import ExitStack

import concourse.mybir as mybir
from concourse.masks import make_identity

F32 = mybir.dt.float32
BF16 = mybir.dt.bfloat16
U32 = mybir.dt.uint32
U8 = mybir.dt.uint8
FP8X4 = mybir.dt.float8_e4m3fn_x4
ACT = mybir.ActivationFunctionType
ALU = mybir.AluOpType

P = 128
BATCH, IN_Q, OUT_Q = 8192, 256, 128
K, N = 4 * IN_Q, 4 * OUT_Q
FLOPS = 2 * BATCH * K * N
ROW_TILES = BATCH // P
R = 2
GROUPS = ROW_TILES // R
STORE_GROUPS = 2
HEAD_CHUNKS = [1, 1, 2, 4, 4, 4]
MAIN_CHUNK = 8
MAIN_BUFS = 4
LAG_MX = 3
LAG_ADD = 4
LAG_TANH = 5
OUT_TILES = STORE_GROUPS * R
SYNC_FROM = 20
FINE_FROM = 52
SPLIT_FROM = 56
WARM_FIRST = 5

PLACE = [
    (0, 0, 1, 1, 0, 1.0),
    (0, 1, 3, 1, 1, -1.0),
    (1, 1, 2, 2, 0, 1.0),
    (1, 0, 1, 1, 1, 1.0),
    (1, 2, 1, 1, 3, -1.0),
    (2, 0, 2, 1, 2, 1.0),
    (2, 2, 1, 1, 0, 1.0),
    (2, 3, 1, 1, 1, -1.0),
    (3, 0, 1, 1, 3, 1.0),
    (3, 1, 1, 1, 2, -1.0),
    (3, 2, 1, 1, 1, 1.0),
    (3, 3, 1, 1, 0, 1.0),
]


def vector_copies(j, r):
    return r == R - 1 and j % 8 in (1, 4, 6) and j > 4


def tile_quatnetpytorchdenselayer_t_kernel(tc, x, W, B, out):
    nc = tc.nc
    xv = x.rearrange("(p t) i c -> p t (i c)", t=ROW_TILES)
    ov = out.rearrange("(p t) o d -> p t (o d)", t=ROW_TILES)

    with ExitStack() as ctx:
        const = ctx.enter_context(tc.tile_pool(name="const", bufs=1))
        xhead = ctx.enter_context(tc.tile_pool(name="xhead", bufs=1))
        xmain = ctx.enter_context(tc.tile_pool(name="xmain", bufs=MAIN_BUFS))
        gpool = ctx.enter_context(tc.tile_pool(name="gpool", bufs=4))
        cpool = ctx.enter_context(tc.tile_pool(name="cpool", bufs=LAG_MX + 3))
        opool = ctx.enter_context(tc.tile_pool(name="opool", bufs=8))
        ps_t = ctx.enter_context(tc.psum_pool(name="ps_t", bufs=4))
        ps_o = ctx.enter_context(tc.psum_pool(name="ps_o", bufs=4))
        ctx.enter_context(tc.manual_schedule())

        ones = const.tile([P, P], BF16, name="ones")
        nc.vector.memset(ones[:], 1.0)
        zeros = const.tile([P, N], BF16, name="zeros")
        nc.vector.memset(zeros[:], 0.0)
        warm = const.tile([P, 1], F32, name="warm")
        nc.vector.memset(warm[:], 0.0)
        b_row = const.tile([P, N], BF16, name="b_row")
        nc.vector.memset(b_row[:], 0.0)
        nc.scalar.activation(out=warm[:], in_=warm[:], func=ACT.Tanh)
        ident = const.tile([P, P], F32, name="ident")
        make_identity(nc, ident[:])

        w_sb = const.tile([P, IN_Q, 4], BF16, name="w_sb")
        nc.sync.dma_start(out=w_sb[:], in_=W)

        chunks = []
        t0 = 0
        for n_rows in HEAD_CHUNKS:
            chunks.append((t0, n_rows))
            t0 += n_rows
        while t0 < ROW_TILES:
            chunks.append((t0, MAIN_CHUNK))
            t0 += MAIN_CHUNK
        where = {}

        def load_chunk(ci):
            first, n_rows = chunks[ci]
            if ci < len(HEAD_CHUNKS):
                xs = xhead.tile([P, n_rows, K], BF16, name="xh%d" % ci)
            else:
                xs = xmain.tile([P, MAIN_CHUNK, K], BF16, name="xs", tag="xs")
            nc.sync.dma_start(out=xs[:], in_=xv[:, first : first + n_rows, :])
            words = xs[:].bitcast(F32)
            for r in range(n_rows):
                where[first + r] = (words, r)

        n_first = len(HEAD_CHUNKS) + MAIN_BUFS
        for ci in range(min(n_first, len(chunks))):
            load_chunk(ci)
            if ci == 2:
                nc.sync.dma_start(out=b_row[0:1, :], in_=B.rearrange("(a o) d -> a (o d)", a=1))
        last_of_chunk = {}
        for ci in range(len(HEAD_CHUNKS), len(chunks)):
            last_of_chunk[chunks[ci][0] + chunks[ci][1] - 1] = ci

        banks = {}
        grouped = {}
        codes = {}
        planes = {}
        accs = {}
        outs = {}

        def keep_clock(bank, times):
            for i_warm in range(times):
                nc.tensor.matmul(out=bank[:].rearrange("p q b -> p (q b)"), lhsT=ones[:], rhs=zeros[:], start=True, stop=True)

        def transposes(j, warmers=0):
            for r in range(R):
                words, idx = where[j * R + r]
                xt = ps_t.tile([P, 4, P], F32, name="xt", tag="xt")
                if r == 0:
                    keep_clock(xt, warmers)
                for q in range(4):
                    nc.tensor.transpose(xt[:, q, :], words[:, idx, q * P : (q + 1) * P], ident[:])
                banks[(j, r)] = xt
                ci = last_of_chunk.get(j * R + r)
                if ci is not None and ci + MAIN_BUFS < len(chunks):
                    load_chunk(ci + MAIN_BUFS)

        def copies(j):
            grp = gpool.tile([P, R * K], BF16, name="grp", tag="grp", align_bytes=64)
            grouped[j] = grp
            gw = grp[:].bitcast(F32).rearrange("p (r g b u) -> p r g b u", r=R, g=2, u=2)
            for r in range(R):
                src = banks[(j, r)][:].rearrange("p (g u) b -> p g b u", u=2)
                if vector_copies(j, r):
                    nc.vector.tensor_copy(out=gw[:, r], in_=src)
                else:
                    nc.scalar.copy(out=gw[:, r], in_=src)

        def quantise(j):
            cw = cpool.tile([P, R * 2 * P], U32, name="cw", tag="cw", align_bytes=64)
            sc = cpool.tile([P, R * 2 * P], U8, name="sc", tag="sc", align_bytes=64)
            nc.vector.quantize_mx(out=cw[:].bitcast(FP8X4), scales=sc[:], in_=grouped[j][:])
            codes[j] = cw
            planes[j] = sc

        def passes(j):
            for r in range(R):
                acc = ps_o.tile([P, N], F32, name="acc", tag="acc")
                for g in range(2):
                    col = (2 * r + g) * P
                    nc.tensor.matmul_mx(
                        out=acc[:],
                        lhsT=codes[j][:, col : col + P].bitcast(FP8X4),
                        lhsT_scale=planes[j][:, col : col + P],
                        rhs=mk_codes[:, g * N : (g + 1) * N].bitcast(FP8X4),
                        rhs_scale=mk_planes[:, g * N : (g + 1) * N],
                        start=(g == 0),
                        stop=(g == 1),
                    )
                accs[(j, r)] = acc

        def adds(j):
            big, half = divmod(j, STORE_GROUPS)
            if half == 0:
                outs[big] = opool.tile([P, STORE_GROUPS * R, N], F32, name="ot", tag="ot")
            for r in range(R):
                nc.vector.tensor_tensor(out=outs[big][:, half * R + r, :], in0=accs[(j, r)][:], in1=bias[:], op=ALU.add)

        def finish(j):
            first = j * R
            big, pos = divmod(first, OUT_TILES)
            pieces = [(first + r, 1) for r in range(R)] if first >= SPLIT_FROM else [(first, R)]
            for t, n_rows in pieces:
                part = outs[big][:, t - big * OUT_TILES : t - big * OUT_TILES + n_rows, :]
                nc.scalar.activation(out=part, in_=part, func=ACT.Tanh)
                if t >= FINE_FROM:
                    nc.sync.dma_start(out=ov[:, t : t + n_rows, :], in_=part)
            if first < FINE_FROM and pos + R == OUT_TILES:
                queue = nc.sync if first >= SYNC_FROM else nc.gpsimd
                queue.dma_start(out=ov[:, big * OUT_TILES : (big + 1) * OUT_TILES, :], in_=outs[big][:])

        mk_t = const.tile([P, 4, K], BF16, name="mk_t")
        mk_v = mk_t[:].rearrange("p d (i c) -> p d i c", c=4)
        for d, c_out, n_c, step, c_in, sign in PLACE:
            dst = mk_v[:, d, :, c_out : c_out + (n_c - 1) * step + 1 : step]
            src = w_sb[:, :, c_in : c_in + (n_c - 1) * step + 1 : step]
            if d < 3:
                nc.vector.tensor_scalar(out=dst, in0=src, scalar1=sign, scalar2=None, op0=ALU.mult)
            else:
                nc.gpsimd.tensor_scalar(out=dst, in0=src, scalar1=sign, scalar2=0.0, op0=ALU.mult, op1=ALU.add)

        transposes(0, WARM_FIRST)
        copies(0)
        transposes(1, 1)
        copies(1)

        pb = ps_o.tile([P, N], F32, name="acc", tag="acc")
        nc.tensor.matmul(out=pb[:], lhsT=ones[:], rhs=b_row[:], start=True, stop=True)
        bias = const.tile([P, N], F32, name="bias")

        mk_w = mk_t[:].bitcast(F32)
        mk_g = const.tile([P, 2, 4 * N], BF16, name="mk_g", align_bytes=64)
        mk_gw = mk_g[:].bitcast(F32).rearrange("p g (o d u) -> p g o d u", d=4, u=2)
        mk_codes = const.tile([P, 2 * N], U32, name="mk_codes", align_bytes=64)
        mk_planes = const.tile([P, 2 * N], U8, name="mk_planes", align_bytes=64)
        mk_banks = {}
        for dh in range(2):
            for g in range(2):
                if (g, dh) == (1, 1):
                    nc.vector.tensor_copy(out=bias[:], in_=pb[:])
                pm = ps_o.tile([P, 4, P], F32, name="acc", tag="acc")
                if (g, dh) == (0, 1):
                    keep_clock(pm, 1)
                for dl in range(2):
                    for u in range(2):
                        first = (2 * g + u) * P
                        nc.tensor.transpose(pm[:, 2 * dl + u, :], mk_w[:, 2 * dh + dl, first : first + P], ident[:])
                mk_banks[(g, dh)] = pm

        def mk_exit(g, dh):
            dst = mk_gw[:, g, :, 2 * dh : 2 * dh + 2, :]
            src = mk_banks[(g, dh)][:].rearrange("p (l u) o -> p o l u", u=2)
            if g == 0:
                nc.vector.tensor_copy(out=dst, in_=src)
            else:
                nc.scalar.copy(out=dst, in_=src)

        mk_exit(0, 0)
        mk_exit(1, 0)
        quantise(0)
        mk_exit(0, 1)
        mk_exit(1, 1)
        for g in range(2):
            nc.vector.quantize_mx(
                out=mk_codes[:, g * N : (g + 1) * N].bitcast(FP8X4),
                scales=mk_planes[:, g * N : (g + 1) * N],
                in_=mk_g[:, g, :],
            )

        for s in range(2, GROUPS + LAG_TANH):
            if s < GROUPS:
                transposes(s, 1 if s <= LAG_MX else 0)
            if 0 <= s - LAG_MX < GROUPS:
                passes(s - LAG_MX)
            if 0 <= s - LAG_ADD < GROUPS:
                adds(s - LAG_ADD)
            if 0 <= s - LAG_TANH < GROUPS:
                finish(s - LAG_TANH)
            if s < GROUPS:
                copies(s)
            if s - 1 < GROUPS:
                quantise(s - 1)
